import numpy as np
import ml_dtypes


BF16 = ml_dtypes.bfloat16


def bf(x):
    return np.asarray(x, np.float32).astype(BF16)


def f64(x):
    return np.asarray(x).astype(np.float64)


E2M1 = np.array([0.0, 0.5, 1.0, 1.5, 2.0, 3.0, 4.0, 6.0, -0.0, -0.5, -1.0, -1.5, -2.0, -3.0, -4.0, -6.0])


def pack_weight(w, fmt):
    k, n = w.shape
    w = f64(bf(w)).reshape(k // 32, 32, n)
    amax = np.abs(w).max(1)
    if fmt == "e4m3":
        byte = np.frexp(amax)[1] - 1 + 127 - 7
    else:
        mant, ex = np.frexp(amax / 6.0)
        byte = np.where(mant > 0.5, ex, ex - 1) + 127
    byte = np.clip(np.where(amax > 0, byte, 1), 1, 254)
    scaled = (w * np.exp2(127.0 - byte)[:, None, :]).reshape(k, n).astype(np.float32)
    by_word = np.ascontiguousarray(scaled.reshape(k // 512, 128, 4, n).transpose(0, 1, 3, 2))
    if fmt == "e4m3":
        words = by_word.astype(ml_dtypes.float8_e4m3fn).view(np.uint8)
    else:
        c = by_word.astype(ml_dtypes.float4_e2m1fn).view(np.uint8) & 0xF
        words = c[..., 0::2] | (c[..., 1::2] << 4)
    return np.ascontiguousarray(words), np.ascontiguousarray(byte.astype(np.uint8).reshape(k // 512, 16, n))


def unpack_weight(words, scales, fmt):
    g, p, n, _ = words.shape
    if fmt == "e4m3":
        vals = np.ascontiguousarray(words).view(ml_dtypes.float8_e4m3fn).astype(np.float64)
    else:
        nib = np.empty((g, p, n, 4), np.uint8)
        nib[..., 0::2] = words & 0xF
        nib[..., 1::2] = words >> 4
        vals = E2M1[nib]
    vals = vals * np.repeat(np.exp2(scales.astype(np.float64) - 127.0), 8, axis=1)[..., None]
    return vals.transpose(0, 1, 3, 2).reshape(g * 512, n)

def pack4(w):
    words, scales = pack_weight(w, "e2m1")
    return words.reshape(words.shape[0], 128, -1), scales


def unpack4(words, scales):
    return unpack_weight(words.reshape(words.shape[0], 128, -1, 2), scales, "e2m1")


def kspread(k):
    return np.exp2(np.repeat(np.random.randint(-6, 7, k // 32), 32).astype(np.float64))


B, S, H, NH, NKV, HD = 1, 512, 1024, 16, 4, 128
NT = NH + 2 * NKV
ROPE_THETA = 10000.0


def rope(t, cos, sin):
    t2 = t.reshape(t.shape[:-1] + (HD // 2, 2))
    t0, t1 = t2[..., 0], t2[..., 1]
    c = cos[None, :, None, :]
    s = sin[None, :, None, :]
    r0 = t0 * c - t1 * s
    r1 = t0 * s + t1 * c
    return np.stack([r0, r1], axis=-1).reshape(t.shape)


def setup_inputs():
    s = kspread(H)
    inv_freq = 1.0 / (ROPE_THETA ** (np.arange(0, HD, 2) / HD))
    freqs = np.outer(np.arange(S), inv_freq)
    x = np.random.standard_normal((B, S, H)) * s
    x_words, x_scales = pack4(x.reshape(B * S, H).T)
    words, scales = pack4(np.random.standard_normal((H, NT * HD)) / np.sqrt(H) / s[:, None])
    return {"x_words": x_words, "x_scales": x_scales,
            "w_qkv_words": words, "w_qkv_scales": scales,
            "cos": bf(np.cos(freqs)), "sin": bf(np.sin(freqs))}


def reference(x_words, x_scales, w_qkv_words, w_qkv_scales, cos, sin):
    xqkv = (unpack4(x_words, x_scales).T.reshape(B, S, H) @ unpack4(w_qkv_words, w_qkv_scales)).reshape(B, S, NT, HD)
    xq = xqkv[:, :, :NH]
    xk = xqkv[:, :, NH:NH + NKV]
    xv = xqkv[:, :, NH + NKV:]
    return rope(xq, f64(cos), f64(sin)), rope(xk, f64(cos), f64(sin)), xv

@@ -1,0 +1,146 @@
+from contextlib import ExitStack
+
+import concourse.mybir as mybir
+
+F32 = mybir.dt.float32
+BF16 = mybir.dt.bfloat16
+U8 = mybir.dt.uint8
+I32 = mybir.dt.int32
+FP4X4 = mybir.dt.float4_e2m1fn_x4
+ADD = mybir.AluOpType.add
+MULT = mybir.AluOpType.mult
+COPY = mybir.ActivationFunctionType.Copy
+
+P = 128
+TOKENS, K, CHANNELS = 512, 1024, 3072
+PASSES = K // 512
+TB = TOKENS // P
+HD = 128
+BANK = 512
+HEADS_PER_BANK = BANK // HD
+FLOPS = 2 * TOKENS * K * CHANNELS
+
+CHUNKS = ((0, 512), (512, 1024), (1536, 1536))
+ORDER = (0, 1, 2, 5, 3, 4)
+
+
+def tile_quantllamaattentionfused_pa_kernel(
+    tc, x_words, x_scales, w_words, w_scales, cos, sin, out_q, out_k, out_v
+):
+    nc = tc.nc
+    q_rows = out_q.rearrange("b s h d -> (b s) (h d)")
+    k_rows = out_k.rearrange("b s h d -> (b s) (h d)")
+    v_rows = out_v.rearrange("b s h d -> (b s) (h d)")
+
+    with ExitStack() as ctx:
+        ctx.enter_context(tc.manual_schedule())
+        keep = ctx.enter_context(tc.tile_pool(name="keep", bufs=1))
+        prods = ctx.enter_context(tc.tile_pool(name="prods", bufs=8))
+        results = ctx.enter_context(tc.tile_pool(name="results", bufs=14))
+        psum = ctx.enter_context(tc.psum_pool(name="psum", bufs=8))
+
+        def load_codes(name, src, first, width):
+            codes = keep.tile([P, PASSES, 2 * width], U8, name=name, align_bytes=64)
+            nc.sync.dma_start(
+                out=codes[:].bitcast(I32),
+                in_=src[:, :, 2 * first : 2 * (first + width)].rearrange("g p c -> p g c").bitcast(I32),
+            )
+            return codes
+
+        def load_scales(planes, src, first, width):
+            for r in range(4):
+                nc.sync.dma_start(
+                    out=planes[r : P : 32, :, :].bitcast(I32),
+                    in_=src[:, r : 16 : 4, first : first + width].rearrange("g q c -> q g c").bitcast(I32),
+                )
+
+        cos_sb = keep.tile([P, TB, HD // 2], BF16, name="cos_sb")
+        sin_sb = keep.tile([P, TB, HD // 2], BF16, name="sin_sb")
+        nc.gpsimd.dma_start(out=cos_sb[:], in_=cos.rearrange("(b p) j -> p b j", p=P))
+        nc.gpsimd.dma_start(out=sin_sb[:], in_=sin.rearrange("(b p) j -> p b j", p=P))
+
+        x_planes = keep.tile([P, PASSES, TOKENS], U8, name="x_planes", align_bytes=64)
+        w_planes = [
+            keep.tile([P, PASSES, width], U8, name="w_planes%d" % i, align_bytes=64)
+            for i, (first, width) in enumerate(CHUNKS)
+        ]
+        warm = keep.tile([P, 1], F32, name="warm")
+        nc.vector.memset(x_planes[:].bitcast(I32), 0)
+        nc.vector.memset(w_planes[0][:].bitcast(I32), 0)
+        nc.vector.memset(warm[:], 0.0)
+        nc.vector.memset(w_planes[1][:].bitcast(I32), 0)
+        nc.vector.memset(w_planes[2][:].bitcast(I32), 0)
+        nc.scalar.activation(out=warm[:], in_=warm[:], func=COPY, scale=1.0)
+
+        x_first = load_codes("x_first", x_words, 0, P)
+        w_codes = [load_codes("w_codes0", w_words, CHUNKS[0][0], CHUNKS[0][1])]
+        load_scales(x_planes, x_scales, 0, TOKENS)
+        load_scales(w_planes[0], w_scales, CHUNKS[0][0], CHUNKS[0][1])
+        x_rest = load_codes("x_rest", x_words, P, TOKENS - P)
+        for i in (1, 2):
+            first, width = CHUNKS[i]
+            w_codes.append(load_codes("w_codes%d" % i, w_words, first, width))
+            load_scales(w_planes[i], w_scales, first, width)
+
+        tables = []
+        for b in range(TB):
+            table = keep.tile([P, 2, HD // 2, 2], F32, name="table%d" % b)
+            nc.scalar.activation(
+                out=table[:, 0, :, :],
+                in_=cos_sb[:, b, :].unsqueeze(2).to_broadcast([P, HD // 2, 2]),
+                func=COPY,
+                scale=1.0,
+            )
+            nc.scalar.activation(out=table[:, 1, :, 0], in_=sin_sb[:, b, :], func=COPY, scale=1.0)
+            nc.scalar.activation(out=table[:, 1, :, 1], in_=sin_sb[:, b, :], func=COPY, scale=-1.0)
+            tables.append(table)
+
+        def chunk_of(n):
+            for i, (first, width) in enumerate(CHUNKS):
+                if first <= n * BANK < first + width:
+                    return i, n * BANK - first
+
+        def project(n, b):
+            i, col = chunk_of(n)
+            acc = psum.tile([P, BANK], F32, name="acc")
+            codes, tok = (x_first, 0) if b == 0 else (x_rest, (b - 1) * P)
+            for g in range(PASSES):
+                nc.tensor.matmul_mx(
+                    out=acc[:],
+                    lhsT=codes[:, g, 2 * tok : 2 * (tok + P)].bitcast(FP4X4),
+                    lhsT_scale=x_planes[:, g, b * P : (b + 1) * P],
+                    rhs=w_codes[i][:, g, 2 * col : 2 * (col + BANK)].bitcast(FP4X4),
+                    rhs_scale=w_planes[i][:, g, col : col + BANK],
+                    start=(g == 0),
+                    stop=(g == PASSES - 1),
+                )
+            return acc
+
+        for n in ORDER:
+            for b in range(TB):
+                acc = project(n, b)
+                res = results.tile([P, BANK], F32, name="res")
+                if n == 5:
+                    nc.scalar.activation(out=res[:], in_=acc[:], func=COPY, scale=1.0)
+                    dst = v_rows[b * P : (b + 1) * P, :]
+                else:
+                    prod = prods.tile([P, 2, BANK], F32, name="prod")
+                    nc.vector.tensor_tensor(
+                        out=prod[:].rearrange("p k (h d) -> p k h d", d=HD),
+                        in0=acc[:].rearrange("p (h d) -> p h d", d=HD).unsqueeze(1).to_broadcast([P, 2, HEADS_PER_BANK, HD]),
+                        in1=tables[b][:].rearrange("p k j e -> p k (j e)").unsqueeze(2).to_broadcast([P, 2, HEADS_PER_BANK, HD]),
+                        op=MULT,
+                    )
+                    last = n == ORDER[-1] and b == TB - 1
+                    engine = nc.vector if last else nc.gpsimd
+                    engine.tensor_tensor(
+                        out=res[:].rearrange("p (j e) -> p j e", e=2),
+                        in0=prod[:, 0, :].rearrange("p (j e) -> p j e", e=2),
+                        in1=prod[:, 1, :].rearrange("p (j e) -> p j e", e=2)[:, :, ::-1],
+                        op=ADD,
+                    )
+                    if n < 4:
+                        dst = q_rows[b * P : (b + 1) * P, n * BANK : (n + 1) * BANK]
+                    else:
+                        dst = k_rows[b * P : (b + 1) * P, :]
+                nc.sync.dma_start(out=dst, in_=res[:])

@@ -1,6 +1,7 @@
 from contextlib import ExitStack
 
 import concourse.mybir as mybir
+from concourse.masks import make_identity
 
 F32 = mybir.dt.float32
 BF16 = mybir.dt.bfloat16
@@ -35,9 +36,11 @@ def tile_quantllamaattentionfused_pa_kernel(
     with ExitStack() as ctx:
         ctx.enter_context(tc.manual_schedule())
         keep = ctx.enter_context(tc.tile_pool(name="keep", bufs=1))
-        prods = ctx.enter_context(tc.tile_pool(name="prods", bufs=8))
-        results = ctx.enter_context(tc.tile_pool(name="results", bufs=14))
-        psum = ctx.enter_context(tc.psum_pool(name="psum", bufs=8))
+        prods = ctx.enter_context(tc.tile_pool(name="prods", bufs=6))
+        results = ctx.enter_context(tc.tile_pool(name="results", bufs=10))
+        psum = ctx.enter_context(tc.psum_pool(name="psum", bufs=7))
+
+        sums = ctx.enter_context(tc.psum_pool(name="sums", bufs=1))
 
         def load_codes(name, src, first, width):
             codes = keep.tile([P, PASSES, 2 * width], U8, name=name, align_bytes=64)
@@ -64,10 +67,17 @@ def tile_quantllamaattentionfused_pa_kernel(
             keep.tile([P, PASSES, width], U8, name="w_planes%d" % i, align_bytes=64)
             for i, (first, width) in enumerate(CHUNKS)
         ]
+        ident = keep.tile([P, P], F32, name="ident")
+        make_identity(nc, ident[:])
         warm = keep.tile([P, 1], F32, name="warm")
         nc.vector.memset(x_planes[:].bitcast(I32), 0)
         nc.vector.memset(w_planes[0][:].bitcast(I32), 0)
         nc.vector.memset(warm[:], 0.0)
+        zeros = keep.tile([P, BANK], BF16, name="zeros")
+        nc.vector.memset(zeros[:], 0.0)
+        idle = sums.tile([P, BANK], F32, name="total")
+        for i in range(7):
+            nc.tensor.matmul(idle[:], lhsT=zeros[:, 0:P], rhs=zeros[:], start=True, stop=True)
         nc.vector.memset(w_planes[1][:].bitcast(I32), 0)
         nc.vector.memset(w_planes[2][:].bitcast(I32), 0)
         nc.scalar.activation(out=warm[:], in_=warm[:], func=COPY, scale=1.0)
@@ -116,31 +126,98 @@ def tile_quantllamaattentionfused_pa_kernel(
                 )
             return acc
 
-        for n in ORDER:
-            for b in range(TB):
-                acc = project(n, b)
-                res = results.tile([P, BANK], F32, name="res")
-                if n == 5:
-                    nc.scalar.activation(out=res[:], in_=acc[:], func=COPY, scale=1.0)
-                    dst = v_rows[b * P : (b + 1) * P, :]
+        def products(b, acc, prod):
+            nc.vector.tensor_tensor(
+                out=prod.rearrange("p k (h d) -> p k h d", d=HD),
+                in0=acc.rearrange("p (h d) -> p h d", d=HD).unsqueeze(1).to_broadcast([P, 2, HEADS_PER_BANK, HD]),
+                in1=tables[b][:].rearrange("p k j e -> p k (j e)").unsqueeze(2).to_broadcast([P, 2, HEADS_PER_BANK, HD]),
+                op=MULT,
+            )
+
+        def one_product(engine, b, u, out, k):
+            engine.tensor_tensor(
+                out=out.rearrange("p (h d) -> p h d", d=HD),
+                in0=u.rearrange("p (h d) -> p h d", d=HD),
+                in1=tables[b][:, k, :, :].rearrange("p j e -> p (j e)").unsqueeze(1).to_broadcast([P, HEADS_PER_BANK, HD]),
+                op=MULT,
+            )
+
+        def add(engine, res, prod):
+            engine.tensor_tensor(
+                out=res.rearrange("p m (j e) -> p m j e", e=2),
+                in0=prod[:, :, 0, :].rearrange("p m (j e) -> p m j e", e=2),
+                in1=prod[:, :, 1, :].rearrange("p m (j e) -> p m j e", e=2)[:, :, :, ::-1],
+                op=ADD,
+            )
+
+        def tensor_add(res, prod):
+            total = sums.tile([P, BANK], F32, name="total")
+            nc.tensor.matmul(total[:], lhsT=ident[:], rhs=prod[:, 0, :], start=True, stop=False)
+            nc.tensor.matmul(
+                total[:], lhsT=ident[:], rhs=prod[:, 1, :].rearrange("p (j e) -> p j e", e=2)[:, :, ::-1], start=False, stop=True
+            )
+            nc.scalar.activation(out=res, in_=total[:], func=COPY, scale=1.0)
+
+        def store(rows, first_col, b, banks, res):
+            nc.sync.dma_start(
+                out=rows[b * P : (b + banks) * P, first_col : first_col + BANK].rearrange("(m p) c -> p m c", p=P),
+                in_=res,
+            )
+
+        GROUPS = (("G",0,1,),("G",1,1,),("G",2,1,),("G",3,1,),("G",4,2,),("G",6,1,),("T",7,1,),("G",8,1,),("G",9,1,),("G",10,1,),("T",11,1,),("G",12,1,),("G",13,1,),("G",14,1,),("G",15,1,),("T",16,1,),("G",17,1,),("G",18,1,),("V",19,1,),)
+        VALUES_AFTER = [8,10,12,14]
+        GPROD = []
+        seq = []
+        values = 0
+        for i in range(20):
+            seq.append((i // 4, i % 4))
+            if i in VALUES_AFTER:
+                seq.append((5, values))
+                values += 1
+        accs = {}
+        state = [0]
+
+        def project_until(n, b):
+            stop = min(len(seq), seq.index((n, b)) + 1 + 6)
+            while state[0] < stop:
+                key = seq[state[0]]
+                accs[key] = project(key[0], key[1])
+                if key[0] == 5:
+                    res = results.tile([P, 2, BANK], F32, name="res")
+                    nc.scalar.activation(out=res[:, 0, :], in_=accs[key][:], func=COPY, scale=1.0)
+                    store(v_rows, 0, key[1], 1, res[:, 0:1, :])
+                state[0] += 1
+
+        pending = []
+        for kind, first, banks in GROUPS:
+            n, b = first // 4, first % 4
+            rows, col = (q_rows, n * BANK) if n < 4 else (k_rows, 0)
+            res = results.tile([P, 2, BANK], F32, name="res")
+            prod = prods.tile([P, 2, 2, BANK], F32, name="prod")
+            for m in range(banks):
+                project_until(n, b + m)
+                acc = accs[(n, b + m)]
+                if first + m in GPROD:
+                    u = prods.tile([P, BANK], F32, name="u")
+                    nc.scalar.activation(out=u[:], in_=acc[:], func=COPY, scale=1.0)
+                    one_product(nc.vector, b + m, acc[:], prod[:, m, 0, :], 0)
+                    one_product(nc.gpsimd, b + m, u[:], prod[:, m, 1, :], 1)
                 else:
-                    prod = prods.tile([P, 2, BANK], F32, name="prod")
-                    nc.vector.tensor_tensor(
-                        out=prod[:].rearrange("p k (h d) -> p k h d", d=HD),
-                        in0=acc[:].rearrange("p (h d) -> p h d", d=HD).unsqueeze(1).to_broadcast([P, 2, HEADS_PER_BANK, HD]),
-                        in1=tables[b][:].rearrange("p k j e -> p k (j e)").unsqueeze(2).to_broadcast([P, 2, HEADS_PER_BANK, HD]),
-                        op=MULT,
+                    products(b + m, acc[:], prod[:, m, :, :])
+            if kind == "T":
+                pending.append((rows, col, b, res, prod))
+            elif kind == "V":
+                half = BANK // 2
+                for c in (0, half):
+                    add(nc.vector, res[:, 0:1, c : c + half], prod[:, 0:1, :, c : c + half])
+                    nc.sync.dma_start(
+                        out=rows[b * P : (b + 1) * P, col + c : col + c + half], in_=res[:, 0, c : c + half]
                     )
-                    last = n == ORDER[-1] and b == TB - 1
-                    engine = nc.vector if last else nc.gpsimd
-                    engine.tensor_tensor(
-                        out=res[:].rearrange("p (j e) -> p j e", e=2),
-                        in0=prod[:, 0, :].rearrange("p (j e) -> p j e", e=2),
-                        in1=prod[:, 1, :].rearrange("p (j e) -> p j e", e=2)[:, :, ::-1],
-                        op=ADD,
-                    )
-                    if n < 4:
-                        dst = q_rows[b * P : (b + 1) * P, n * BANK : (n + 1) * BANK]
-                    else:
-                        dst = k_rows[b * P : (b + 1) * P, :]
-                nc.sync.dma_start(out=dst, in_=res[:])
+            else:
+                add(nc.gpsimd, res[:, 0:banks, :], prod[:, 0:banks, :, :])
+                store(rows, col, b, banks, res[:, 0:banks, :])
+            if kind != "T" and pending:
+                rows, col, b, res, prod = pending[0]
+                pending.clear()
+                tensor_add(res[:, 0, :], prod[:, 0, :, :])
+                store(rows, col, b, 1, res[:, 0:1, :])

@@ -38,9 +38,9 @@ def tile_quantllamaattentionfused_pa_kernel(
         keep = ctx.enter_context(tc.tile_pool(name="keep", bufs=1))
         prods = ctx.enter_context(tc.tile_pool(name="prods", bufs=6))
         results = ctx.enter_context(tc.tile_pool(name="results", bufs=10))
-        psum = ctx.enter_context(tc.psum_pool(name="psum", bufs=7))
+        psum = ctx.enter_context(tc.psum_pool(name="psum", bufs=6))
 
-        sums = ctx.enter_context(tc.psum_pool(name="sums", bufs=1))
+        sums = ctx.enter_context(tc.psum_pool(name="sums", bufs=2))
 
         def load_codes(name, src, first, width):
             codes = keep.tile([P, PASSES, 2 * width], U8, name=name, align_bytes=64)
@@ -93,7 +93,8 @@ def tile_quantllamaattentionfused_pa_kernel(
             load_scales(w_planes[i], w_scales, first, width)
 
         tables = []
-        for b in range(TB):
+
+        def make_table(b):
             table = keep.tile([P, 2, HD // 2, 2], F32, name="table%d" % b)
             nc.scalar.activation(
                 out=table[:, 0, :, :],
@@ -104,6 +105,9 @@ def tile_quantllamaattentionfused_pa_kernel(
             nc.scalar.activation(out=table[:, 1, :, 0], in_=sin_sb[:, b, :], func=COPY, scale=1.0)
             nc.scalar.activation(out=table[:, 1, :, 1], in_=sin_sb[:, b, :], func=COPY, scale=-1.0)
             tables.append(table)
+
+        make_table(0)
+        make_table(1)
 
         def chunk_of(n):
             for i, (first, width) in enumerate(CHUNKS):
@@ -142,6 +146,14 @@ def tile_quantllamaattentionfused_pa_kernel(
                 op=MULT,
             )
 
+        def swapped_product(b, u, out):
+            nc.vector.tensor_tensor(
+                out=out.rearrange("p (h j e) -> p h j e", h=HEADS_PER_BANK, e=2),
+                in0=u.rearrange("p (h j e) -> p h j e", h=HEADS_PER_BANK, e=2)[:, :, :, ::-1],
+                in1=tables[b][:, 1, :, ::-1].unsqueeze(1).to_broadcast([P, HEADS_PER_BANK, HD // 2, 2]),
+                op=MULT,
+            )
+
         def add(engine, res, prod):
             engine.tensor_tensor(
                 out=res.rearrange("p m (j e) -> p m j e", e=2),
@@ -154,7 +166,7 @@ def tile_quantllamaattentionfused_pa_kernel(
             total = sums.tile([P, BANK], F32, name="total")
             nc.tensor.matmul(total[:], lhsT=ident[:], rhs=prod[:, 0, :], start=True, stop=False)
             nc.tensor.matmul(
-                total[:], lhsT=ident[:], rhs=prod[:, 1, :].rearrange("p (j e) -> p j e", e=2)[:, :, ::-1], start=False, stop=True
+                total[:], lhsT=ident[:], rhs=prod[:, 1, :], start=False, stop=True
             )
             nc.scalar.activation(out=res, in_=total[:], func=COPY, scale=1.0)
 
@@ -164,9 +176,9 @@ def tile_quantllamaattentionfused_pa_kernel(
                 in_=res,
             )
 
-        GROUPS = (("G",0,1,),("G",1,1,),("G",2,1,),("G",3,1,),("G",4,2,),("G",6,1,),("T",7,1,),("G",8,1,),("G",9,1,),("G",10,1,),("T",11,1,),("G",12,1,),("G",13,1,),("G",14,1,),("G",15,1,),("T",16,1,),("G",17,1,),("G",18,1,),("V",19,1,),)
-        VALUES_AFTER = [8,10,12,14]
-        GPROD = []
+        GROUPS = (("G",0,2,),("G",2,2,),("G",4,1,),("T",5,1,),("G",6,1,),("G",7,1,),("G",8,2,),("T",10,1,),("G",11,1,),("G",12,1,),("G",13,1,),("G",14,2,),("T",16,1,),("G",17,1,),("L",18,1,),("L",19,1,),)
+        VALUES_AFTER = [6,8,9,10]
+        GPROD = [0]
         seq = []
         values = 0
         for i in range(20):
@@ -178,7 +190,7 @@ def tile_quantllamaattentionfused_pa_kernel(
         state = [0]
 
         def project_until(n, b):
-            stop = min(len(seq), seq.index((n, b)) + 1 + 6)
+            stop = min(len(seq), seq.index((n, b)) + 1 + 5)
             while state[0] < stop:
                 key = seq[state[0]]
                 accs[key] = project(key[0], key[1])
@@ -189,6 +201,7 @@ def tile_quantllamaattentionfused_pa_kernel(
                 state[0] += 1
 
         pending = []
+        late = []
         for kind, first, banks in GROUPS:
             n, b = first // 4, first % 4
             rows, col = (q_rows, n * BANK) if n < 4 else (k_rows, 0)
@@ -199,20 +212,21 @@ def tile_quantllamaattentionfused_pa_kernel(
                 acc = accs[(n, b + m)]
                 if first + m in GPROD:
                     u = prods.tile([P, BANK], F32, name="u")
-                    nc.scalar.activation(out=u[:], in_=acc[:], func=COPY, scale=1.0)
                     one_product(nc.vector, b + m, acc[:], prod[:, m, 0, :], 0)
+                    nc.scalar.activation(out=u[:], in_=acc[:], func=COPY, scale=1.0)
                     one_product(nc.gpsimd, b + m, u[:], prod[:, m, 1, :], 1)
+                    if len(tables) == 2:
+                        make_table(2)
+                        make_table(3)
+                elif kind == "T":
+                    one_product(nc.vector, b, acc[:], prod[:, 0, 0, :], 0)
+                    swapped_product(b, acc[:], prod[:, 0, 1, :])
                 else:
                     products(b + m, acc[:], prod[:, m, :, :])
             if kind == "T":
                 pending.append((rows, col, b, res, prod))
-            elif kind == "V":
-                half = BANK // 2
-                for c in (0, half):
-                    add(nc.vector, res[:, 0:1, c : c + half], prod[:, 0:1, :, c : c + half])
-                    nc.sync.dma_start(
-                        out=rows[b * P : (b + 1) * P, col + c : col + c + half], in_=res[:, 0, c : c + half]
-                    )
+            elif kind == "L":
+                late.append((rows, col, b, res, prod))
             else:
                 add(nc.gpsimd, res[:, 0:banks, :], prod[:, 0:banks, :, :])
                 store(rows, col, b, banks, res[:, 0:banks, :])
@@ -221,3 +235,10 @@ def tile_quantllamaattentionfused_pa_kernel(
                 pending.clear()
                 tensor_add(res[:, 0, :], prod[:, 0, :, :])
                 store(rows, col, b, 1, res[:, 0:1, :])
+        for i, (rows, col, b, res, prod) in enumerate(late):
+            width = BANK // 2 if i == len(late) - 1 else BANK
+            for c in range(0, BANK, width):
+                add(nc.vector, res[:, 0:1, c : c + width], prod[:, 0:1, :, c : c + width])
+                nc.sync.dma_start(
+                    out=rows[b * P : (b + 1) * P, col + c : col + c + width], in_=res[:, 0, c : c + width]
+                )

@@ -59,8 +59,8 @@ def tile_quantllamaattentionfused_pa_kernel(
 
         cos_sb = keep.tile([P, TB, HD // 2], BF16, name="cos_sb")
         sin_sb = keep.tile([P, TB, HD // 2], BF16, name="sin_sb")
-        nc.gpsimd.dma_start(out=cos_sb[:], in_=cos.rearrange("(b p) j -> p b j", p=P))
-        nc.gpsimd.dma_start(out=sin_sb[:], in_=sin.rearrange("(b p) j -> p b j", p=P))
+        nc.scalar.dma_start(out=cos_sb[:], in_=cos.rearrange("(b p) j -> p b j", p=P))
+        nc.scalar.dma_start(out=sin_sb[:], in_=sin.rearrange("(b p) j -> p b j", p=P))
 
         x_planes = keep.tile([P, PASSES, TOKENS], U8, name="x_planes", align_bytes=64)
         w_planes = [
@@ -176,7 +176,7 @@ def tile_quantllamaattentionfused_pa_kernel(
                 in_=res,
             )
 
-        GROUPS = (("G",0,2,),("G",2,2,),("G",4,1,),("T",5,1,),("G",6,1,),("G",7,1,),("G",8,2,),("T",10,1,),("G",11,1,),("G",12,1,),("G",13,1,),("G",14,2,),("T",16,1,),("G",17,1,),("L",18,1,),("L",19,1,),)
+        GROUPS = (("G",0,1,),("G",1,1,),("T",2,1,),("G",3,1,),("G",4,2,),("G",6,2,),("G",8,2,),("G",10,2,),("T",12,1,),("G",13,1,),("G",14,2,),("T",16,1,),("G",17,1,),("L",18,1,),("L",19,1,),)
         VALUES_AFTER = [6,8,9,10]
         GPROD = [0]
         seq = []

from contextlib import ExitStack

import concourse.mybir as mybir
from concourse.masks import make_identity

F32 = mybir.dt.float32
BF16 = mybir.dt.bfloat16
U8 = mybir.dt.uint8
I32 = mybir.dt.int32
FP4X4 = mybir.dt.float4_e2m1fn_x4
ADD = mybir.AluOpType.add
MULT = mybir.AluOpType.mult
COPY = mybir.ActivationFunctionType.Copy

P = 128
TOKENS, K, CHANNELS = 512, 1024, 3072
PASSES = K // 512
TB = TOKENS // P
HD = 128
BANK = 512
HEADS_PER_BANK = BANK // HD
FLOPS = 2 * TOKENS * K * CHANNELS

CHUNKS = ((0, 512), (512, 1024), (1536, 1536))
ORDER = (0, 1, 2, 5, 3, 4)


def tile_quantllamaattentionfused_pa_kernel(
    tc, x_words, x_scales, w_words, w_scales, cos, sin, out_q, out_k, out_v
):
    nc = tc.nc
    q_rows = out_q.rearrange("b s h d -> (b s) (h d)")
    k_rows = out_k.rearrange("b s h d -> (b s) (h d)")
    v_rows = out_v.rearrange("b s h d -> (b s) (h d)")

    with ExitStack() as ctx:
        ctx.enter_context(tc.manual_schedule())
        keep = ctx.enter_context(tc.tile_pool(name="keep", bufs=1))
        prods = ctx.enter_context(tc.tile_pool(name="prods", bufs=6))
        results = ctx.enter_context(tc.tile_pool(name="results", bufs=10))
        psum = ctx.enter_context(tc.psum_pool(name="psum", bufs=6))

        sums = ctx.enter_context(tc.psum_pool(name="sums", bufs=2))

        def load_codes(name, src, first, width):
            codes = keep.tile([P, PASSES, 2 * width], U8, name=name, align_bytes=64)
            nc.sync.dma_start(
                out=codes[:].bitcast(I32),
                in_=src[:, :, 2 * first : 2 * (first + width)].rearrange("g p c -> p g c").bitcast(I32),
            )
            return codes

        def load_scales(planes, src, first, width):
            for r in range(4):
                nc.sync.dma_start(
                    out=planes[r : P : 32, :, :].bitcast(I32),
                    in_=src[:, r : 16 : 4, first : first + width].rearrange("g q c -> q g c").bitcast(I32),
                )

        cos_sb = keep.tile([P, TB, HD // 2], BF16, name="cos_sb")
        sin_sb = keep.tile([P, TB, HD // 2], BF16, name="sin_sb")
        nc.scalar.dma_start(out=cos_sb[:], in_=cos.rearrange("(b p) j -> p b j", p=P))
        nc.scalar.dma_start(out=sin_sb[:], in_=sin.rearrange("(b p) j -> p b j", p=P))

        x_planes = keep.tile([P, PASSES, TOKENS], U8, name="x_planes", align_bytes=64)
        w_planes = [
            keep.tile([P, PASSES, width], U8, name="w_planes%d" % i, align_bytes=64)
            for i, (first, width) in enumerate(CHUNKS)
        ]
        ident = keep.tile([P, P], F32, name="ident")
        make_identity(nc, ident[:])
        warm = keep.tile([P, 1], F32, name="warm")
        nc.vector.memset(x_planes[:].bitcast(I32), 0)
        nc.vector.memset(w_planes[0][:].bitcast(I32), 0)
        nc.vector.memset(warm[:], 0.0)
        zeros = keep.tile([P, BANK], BF16, name="zeros")
        nc.vector.memset(zeros[:], 0.0)
        idle = sums.tile([P, BANK], F32, name="total")
        for i in range(7):
            nc.tensor.matmul(idle[:], lhsT=zeros[:, 0:P], rhs=zeros[:], start=True, stop=True)
        nc.vector.memset(w_planes[1][:].bitcast(I32), 0)
        nc.vector.memset(w_planes[2][:].bitcast(I32), 0)
        nc.scalar.activation(out=warm[:], in_=warm[:], func=COPY, scale=1.0)

        x_first = load_codes("x_first", x_words, 0, P)
        w_codes = [load_codes("w_codes0", w_words, CHUNKS[0][0], CHUNKS[0][1])]
        load_scales(x_planes, x_scales, 0, TOKENS)
        load_scales(w_planes[0], w_scales, CHUNKS[0][0], CHUNKS[0][1])
        x_rest = load_codes("x_rest", x_words, P, TOKENS - P)
        for i in (1, 2):
            first, width = CHUNKS[i]
            w_codes.append(load_codes("w_codes%d" % i, w_words, first, width))
            load_scales(w_planes[i], w_scales, first, width)

        tables = []

        def make_table(b):
            table = keep.tile([P, 2, HD // 2, 2], F32, name="table%d" % b)
            nc.scalar.activation(
                out=table[:, 0, :, :],
                in_=cos_sb[:, b, :].unsqueeze(2).to_broadcast([P, HD // 2, 2]),
                func=COPY,
                scale=1.0,
            )
            nc.scalar.activation(out=table[:, 1, :, 0], in_=sin_sb[:, b, :], func=COPY, scale=1.0)
            nc.scalar.activation(out=table[:, 1, :, 1], in_=sin_sb[:, b, :], func=COPY, scale=-1.0)
            tables.append(table)

        make_table(0)
        make_table(1)

        def chunk_of(n):
            for i, (first, width) in enumerate(CHUNKS):
                if first <= n * BANK < first + width:
                    return i, n * BANK - first

        def project(n, b):
            i, col = chunk_of(n)
            acc = psum.tile([P, BANK], F32, name="acc")
            codes, tok = (x_first, 0) if b == 0 else (x_rest, (b - 1) * P)
            for g in range(PASSES):
                nc.tensor.matmul_mx(
                    out=acc[:],
                    lhsT=codes[:, g, 2 * tok : 2 * (tok + P)].bitcast(FP4X4),
                    lhsT_scale=x_planes[:, g, b * P : (b + 1) * P],
                    rhs=w_codes[i][:, g, 2 * col : 2 * (col + BANK)].bitcast(FP4X4),
                    rhs_scale=w_planes[i][:, g, col : col + BANK],
                    start=(g == 0),
                    stop=(g == PASSES - 1),
                )
            return acc

        def products(b, acc, prod):
            nc.vector.tensor_tensor(
                out=prod.rearrange("p k (h d) -> p k h d", d=HD),
                in0=acc.rearrange("p (h d) -> p h d", d=HD).unsqueeze(1).to_broadcast([P, 2, HEADS_PER_BANK, HD]),
                in1=tables[b][:].rearrange("p k j e -> p k (j e)").unsqueeze(2).to_broadcast([P, 2, HEADS_PER_BANK, HD]),
                op=MULT,
            )

        def one_product(engine, b, u, out, k):
            engine.tensor_tensor(
                out=out.rearrange("p (h d) -> p h d", d=HD),
                in0=u.rearrange("p (h d) -> p h d", d=HD),
                in1=tables[b][:, k, :, :].rearrange("p j e -> p (j e)").unsqueeze(1).to_broadcast([P, HEADS_PER_BANK, HD]),
                op=MULT,
            )

        def swapped_product(b, u, out):
            nc.vector.tensor_tensor(
                out=out.rearrange("p (h j e) -> p h j e", h=HEADS_PER_BANK, e=2),
                in0=u.rearrange("p (h j e) -> p h j e", h=HEADS_PER_BANK, e=2)[:, :, :, ::-1],
                in1=tables[b][:, 1, :, ::-1].unsqueeze(1).to_broadcast([P, HEADS_PER_BANK, HD // 2, 2]),
                op=MULT,
            )

        def add(engine, res, prod):
            engine.tensor_tensor(
                out=res.rearrange("p m (j e) -> p m j e", e=2),
                in0=prod[:, :, 0, :].rearrange("p m (j e) -> p m j e", e=2),
                in1=prod[:, :, 1, :].rearrange("p m (j e) -> p m j e", e=2)[:, :, :, ::-1],
                op=ADD,
            )

        def tensor_add(res, prod):
            total = sums.tile([P, BANK], F32, name="total")
            nc.tensor.matmul(total[:], lhsT=ident[:], rhs=prod[:, 0, :], start=True, stop=False)
            nc.tensor.matmul(
                total[:], lhsT=ident[:], rhs=prod[:, 1, :], start=False, stop=True
            )
            nc.scalar.activation(out=res, in_=total[:], func=COPY, scale=1.0)

        def store(rows, first_col, b, banks, res):
            nc.sync.dma_start(
                out=rows[b * P : (b + banks) * P, first_col : first_col + BANK].rearrange("(m p) c -> p m c", p=P),
                in_=res,
            )

        GROUPS = (("G",0,1,),("G",1,1,),("T",2,1,),("G",3,1,),("G",4,2,),("G",6,2,),("G",8,2,),("G",10,2,),("T",12,1,),("G",13,1,),("G",14,2,),("T",16,1,),("G",17,1,),("L",18,1,),("L",19,1,),)
        VALUES_AFTER = [6,8,9,10]
        GPROD = [0]
        seq = []
        values = 0
        for i in range(20):
            seq.append((i // 4, i % 4))
            if i in VALUES_AFTER:
                seq.append((5, values))
                values += 1
        accs = {}
        state = [0]

        def project_until(n, b):
            stop = min(len(seq), seq.index((n, b)) + 1 + 5)
            while state[0] < stop:
                key = seq[state[0]]
                accs[key] = project(key[0], key[1])
                if key[0] == 5:
                    res = results.tile([P, 2, BANK], F32, name="res")
                    nc.scalar.activation(out=res[:, 0, :], in_=accs[key][:], func=COPY, scale=1.0)
                    store(v_rows, 0, key[1], 1, res[:, 0:1, :])
                state[0] += 1

        pending = []
        late = []
        for kind, first, banks in GROUPS:
            n, b = first // 4, first % 4
            rows, col = (q_rows, n * BANK) if n < 4 else (k_rows, 0)
            res = results.tile([P, 2, BANK], F32, name="res")
            prod = prods.tile([P, 2, 2, BANK], F32, name="prod")
            for m in range(banks):
                project_until(n, b + m)
                acc = accs[(n, b + m)]
                if first + m in GPROD:
                    u = prods.tile([P, BANK], F32, name="u")
                    one_product(nc.vector, b + m, acc[:], prod[:, m, 0, :], 0)
                    nc.scalar.activation(out=u[:], in_=acc[:], func=COPY, scale=1.0)
                    one_product(nc.gpsimd, b + m, u[:], prod[:, m, 1, :], 1)
                    if len(tables) == 2:
                        make_table(2)
                        make_table(3)
                elif kind == "T":
                    one_product(nc.vector, b, acc[:], prod[:, 0, 0, :], 0)
                    swapped_product(b, acc[:], prod[:, 0, 1, :])
                else:
                    products(b + m, acc[:], prod[:, m, :, :])
            if kind == "T":
                pending.append((rows, col, b, res, prod))
            elif kind == "L":
                late.append((rows, col, b, res, prod))
            else:
                add(nc.gpsimd, res[:, 0:banks, :], prod[:, 0:banks, :, :])
                store(rows, col, b, banks, res[:, 0:banks, :])
            if kind != "T" and pending:
                rows, col, b, res, prod = pending[0]
                pending.clear()
                tensor_add(res[:, 0, :], prod[:, 0, :, :])
                store(rows, col, b, 1, res[:, 0:1, :])
        for i, (rows, col, b, res, prod) in enumerate(late):
            width = BANK // 2 if i == len(late) - 1 else BANK
            for c in range(0, BANK, width):
                add(nc.vector, res[:, 0:1, c : c + width], prod[:, 0:1, :, c : c + width])
                nc.sync.dma_start(
                    out=rows[b * P : (b + 1) * P, col + c : col + c + width], in_=res[:, 0, c : c + width]
                )
